import numpy as np
import ml_dtypes


def mxq(x, axis, fmt="e4m3"):
    dtype, down = {"e4m3": (ml_dtypes.float8_e4m3fn, 7), "e5m2": (ml_dtypes.float8_e5m2, 14)}[fmt]
    v = np.moveaxis(np.asarray(x, np.float32).astype(ml_dtypes.bfloat16).astype(np.float64), axis, -1)
    blocks = v.reshape(v.shape[:-1] + (-1, 32))
    amax = np.abs(blocks).max(-1, keepdims=True)
    byte = np.maximum(np.where(amax > 0, np.frexp(amax)[1] - 1 + 127, 0) - down, 1)
    scale = np.exp2(byte - 127.0)
    codes = (blocks / scale).astype(np.float32).astype(dtype).astype(np.float64)
    return np.moveaxis((codes * scale).reshape(v.shape), -1, axis)


WIDE = False


def mx_kscale(k):
    if not WIDE:
        return np.ones(k)
    levels = np.array([20, -20, 10, -10, 0])
    a = np.random.permutation(np.resize(levels, k // 512 * 4)).reshape(k // 512, 4)
    idx = np.arange(k)
    return np.exp2(a[idx // 512, idx % 128 // 32])


BF16 = ml_dtypes.bfloat16


def bf(x):
    return np.asarray(x, np.float32).astype(BF16)


def f64(x):
    return np.asarray(x).astype(np.float64)


B, HH, WW, C, NH, KD, WS, SS = 1, 64, 64, 512, 8, 64, 8, 4
GH, GW, T, F = HH // WS, WW // WS, WS * WS, NH * KD
N = B * GH * GW


def setup_inputs():
    u = mx_kscale(C)
    attn_ctx = np.random.standard_normal((N, T, NH, KD)) * 0.4
    x = np.random.standard_normal((B, HH, WW, C))
    wo = np.random.standard_normal((NH, KD, C)) * 2.0 / np.sqrt(F) / u
    bo = np.random.standard_normal(C) * 0.3
    g = np.random.standard_normal((B, HH, WW, C)) * np.exp2(np.random.randint(-12, 1, (B, HH, WW, 1))) * 4.0 * u
    return {"attn_ctx": bf(attn_ctx), "x": bf(x), "wo": bf(wo), "bo": bf(bo), "grad_out": bf(g)}


def reference(attn_ctx, x, wo, bo, grad_out):
    g = np.roll(f64(grad_out), shift=(-SS, -SS), axis=(1, 2))
    g = g.reshape(B, GH, WS, GW, WS, C).swapaxes(2, 3).reshape(N * T, C)
    go = mxq(g, 1, "e5m2") @ mxq(f64(wo).reshape(F, C), 1, "e4m3").T
    return go.reshape(N, T, NH, KD)

@@ -1,0 +1,141 @@
+from contextlib import ExitStack
+
+import concourse.mybir as mybir
+from concourse.masks import make_identity
+
+BF16 = mybir.dt.bfloat16
+F32 = mybir.dt.float32
+U32 = mybir.dt.uint32
+U8 = mybir.dt.uint8
+E4M3X4 = mybir.dt.float8_e4m3fn_x4
+E5M2X4 = mybir.dt.float8_e5m2_x4
+
+P = 128
+C = 512
+F = 512
+PIXELS = 64 * 64
+WORDS = C // 2
+HALVES = WORDS // P
+PACK = 4
+IR = 4
+SLOTS = 8
+GROUP = 4
+BANK_SLOTS = 2
+
+FLOPS = 2 * PIXELS * C * F
+BYTES = 2 * (PIXELS * C + F * C) + 4 * PIXELS * F
+
+
+def turn_group(nc, banks, words, first_slot, order):
+    turned_banks = []
+    for b in range(GROUP // BANK_SLOTS):
+        turned = banks.tile([P, BANK_SLOTS, HALVES, P], F32, name="turned")
+        for k in range(BANK_SLOTS):
+            slot = first_slot + b * BANK_SLOTS + k
+            for u in range(HALVES):
+                start = slot * WORDS + u * P
+                nc.tensor.transpose(turned[:, k, u, :], words[:, start : start + P], order)
+        turned_banks.append(turned)
+    return turned_banks
+
+
+def regroup(nc, turned_banks, grouped):
+    grouped_words = grouped[:].bitcast(F32)
+    width = BANK_SLOTS * P * HALVES
+    for b, turned in enumerate(turned_banks):
+        nc.vector.tensor_copy(
+            out=grouped_words[:, b * width : (b + 1) * width].rearrange(
+                "p (k t u) -> p k t u", k=BANK_SLOTS, u=HALVES
+            ),
+            in_=turned[:].rearrange("p k u t -> p k t u"),
+        )
+
+
+def tile_windowattentionblock_pb_kernel(tc, attn_ctx, x, wo, bo, grad_out, out):
+    nc = tc.nc
+    image = grad_out.rearrange("b (ib ir) (a s) c -> ir (b ib) a (s c)", ir=IR, s=SLOTS)
+    windows = out.rearrange("n (hi ir tj) h d -> (n hi) ir (tj h d)", hi=2, ir=IR)
+    weight_rows = wo.rearrange("h d c -> (h d) c").rearrange("(r p) c -> p r c", p=P)
+
+    with ExitStack() as stack:
+        stack.enter_context(tc.manual_schedule())
+        const = stack.enter_context(tc.tile_pool(name="const", bufs=1))
+        raw_pool = stack.enter_context(tc.tile_pool(name="raw", bufs=IR))
+        group_pool = stack.enter_context(tc.tile_pool(name="group", bufs=2 * IR))
+        turn_banks = stack.enter_context(tc.psum_pool(name="turn_banks", bufs=4))
+        sum_banks = stack.enter_context(tc.psum_pool(name="sum_banks", bufs=4))
+
+        w_raw = const.tile([P, GROUP * C], BF16)
+        nc.sync.dma_start(out=w_raw[:].rearrange("p (r c) -> p r c", c=C), in_=weight_rows)
+        raw_words = []
+        for ir in range(IR):
+            g_raw = raw_pool.tile([P, SLOTS * C], BF16)
+            nc.sync.dma_start(out=g_raw[:], in_=image[ir])
+            raw_words.append(g_raw[:].bitcast(F32))
+
+        ident2 = const.tile([P, 2 * P], F32)
+        make_identity(nc, ident2[:, 0:P])
+        nc.vector.tensor_copy(out=ident2[:, P : 2 * P], in_=ident2[:, 0:P])
+        identity = ident2[:, 0:P]
+        rotated = ident2[:, 8 : 8 + P].rearrange("p (gi hi a) -> p gi a hi", hi=2, a=8)
+        order_same = const.tile([P, P], F32)
+        nc.vector.tensor_copy(
+            out=order_same[:].rearrange("p (gi gj hi) -> p gi gj hi", gj=8, hi=2), in_=rotated
+        )
+        order_left = const.tile([P, P], F32)
+        left_view = order_left[:].rearrange("p (gi gj hi) -> p gi gj hi", gj=8, hi=2)
+        nc.vector.tensor_copy(out=left_view[:, :, 0:7, :], in_=rotated[:, :, 1:8, :])
+        nc.vector.tensor_copy(out=left_view[:, :, 7:8, :], in_=rotated[:, :, 0:1, :])
+
+        groups = []
+        for ir in range(IR):
+            groups.append((ir, 4, 0, order_same))
+            groups.append((ir, 0, 4, order_left))
+
+        def turn(g):
+            ir, first_slot, first_tj, order = groups[g]
+            return turn_group(nc, turn_banks, raw_words[ir], first_slot, order[:])
+
+        w_turned = turn_group(nc, turn_banks, w_raw[:].bitcast(F32), 0, identity)
+        turned = {0: turn(0)}
+        w_grouped = const.tile([P, F * PACK], BF16, align_bytes=64)
+        regroup(nc, w_turned, w_grouped)
+        turned[1] = turn(1)
+        grouped = {}
+        g_grouped = group_pool.tile([P, GROUP * P * PACK], BF16, align_bytes=64)
+        regroup(nc, turned[0], g_grouped)
+        grouped[0] = g_grouped
+        w_codes = const.tile([P, F], U32, align_bytes=64)
+        w_scales = const.tile([P, F], U8, align_bytes=64)
+        nc.vector.quantize_mx(out=w_codes[:].bitcast(E4M3X4), scales=w_scales[:], in_=w_grouped[:])
+
+        for g in range(len(groups)):
+            ir, first_slot, first_tj, order = groups[g]
+            if g + 2 < len(groups):
+                turned[g + 2] = turn(g + 2)
+            if g + 1 < len(groups):
+                g_grouped = group_pool.tile([P, GROUP * P * PACK], BF16, align_bytes=64)
+                regroup(nc, turned[g + 1], g_grouped)
+                grouped[g + 1] = g_grouped
+            g_codes = group_pool.tile([P, GROUP * P], U32, align_bytes=64)
+            g_scales = group_pool.tile([P, GROUP * P], U8, align_bytes=64)
+            nc.vector.quantize_mx(
+                out=g_codes[:].bitcast(E5M2X4), scales=g_scales[:], in_=grouped[g][:]
+            )
+            result = group_pool.tile([P, GROUP * F], F32)
+            for k in range(GROUP):
+                tokens = slice(k * P, (k + 1) * P)
+                sums = sum_banks.tile([P, F], F32)
+                nc.tensor.matmul_mx(
+                    out=sums[:],
+                    lhsT=g_codes[:, tokens].bitcast(E5M2X4),
+                    lhsT_scale=g_scales[:, tokens],
+                    rhs=w_codes[:].bitcast(E4M3X4),
+                    rhs_scale=w_scales[:],
+                    start=True,
+                    stop=True,
+                )
+                nc.scalar.copy(out=result[:, k * F : (k + 1) * F], in_=sums[:])
+            nc.sync.dma_start(
+                out=windows[:, ir, first_tj * F : (first_tj + GROUP) * F], in_=result[:]
+            )

@@ -17,23 +17,23 @@ PIXELS = 64 * 64
 WORDS = C // 2
 HALVES = WORDS // P
 PACK = 4
-IR = 4
-SLOTS = 8
-GROUP = 4
+WINDOW_ROWS = 8
+BLOCKS = 16
+SLOTS = 4
 BANK_SLOTS = 2
 
 FLOPS = 2 * PIXELS * C * F
 BYTES = 2 * (PIXELS * C + F * C) + 4 * PIXELS * F
 
 
-def turn_group(nc, banks, words, first_slot, order):
+def turn(nc, banks, rows, order):
+    words = rows[:].bitcast(F32)
     turned_banks = []
-    for b in range(GROUP // BANK_SLOTS):
+    for b in range(SLOTS // BANK_SLOTS):
         turned = banks.tile([P, BANK_SLOTS, HALVES, P], F32, name="turned")
         for k in range(BANK_SLOTS):
-            slot = first_slot + b * BANK_SLOTS + k
             for u in range(HALVES):
-                start = slot * WORDS + u * P
+                start = (b * BANK_SLOTS + k) * WORDS + u * P
                 nc.tensor.transpose(turned[:, k, u, :], words[:, start : start + P], order)
         turned_banks.append(turned)
     return turned_banks
@@ -53,78 +53,65 @@ def regroup(nc, turned_banks, grouped):
 
 def tile_windowattentionblock_pb_kernel(tc, attn_ctx, x, wo, bo, grad_out, out):
     nc = tc.nc
-    image = grad_out.rearrange("b (ib ir) (a s) c -> ir (b ib) a (s c)", ir=IR, s=SLOTS)
-    windows = out.rearrange("n (hi ir tj) h d -> (n hi) ir (tj h d)", hi=2, ir=IR)
+    blocks = grad_out.rearrange("b (ib ir) (jb jr) c -> (b ib) (ir jb) (jr c)", ir=4, jr=SLOTS)
+    window_rows = out.rearrange(
+        "(gi gj) (hi ir hj jr) h d -> gi (gj hi ir hj) (jr h d)", gi=WINDOW_ROWS, hi=2, ir=4, hj=2
+    )
     weight_rows = wo.rearrange("h d c -> (h d) c").rearrange("(r p) c -> p r c", p=P)
 
     with ExitStack() as stack:
         stack.enter_context(tc.manual_schedule())
         const = stack.enter_context(tc.tile_pool(name="const", bufs=1))
-        raw_pool = stack.enter_context(tc.tile_pool(name="raw", bufs=IR))
-        group_pool = stack.enter_context(tc.tile_pool(name="group", bufs=2 * IR))
+        work = stack.enter_context(tc.tile_pool(name="work", bufs=WINDOW_ROWS))
         turn_banks = stack.enter_context(tc.psum_pool(name="turn_banks", bufs=4))
         sum_banks = stack.enter_context(tc.psum_pool(name="sum_banks", bufs=4))
 
-        w_raw = const.tile([P, GROUP * C], BF16)
+        w_raw = const.tile([P, SLOTS * C], BF16)
         nc.sync.dma_start(out=w_raw[:].rearrange("p (r c) -> p r c", c=C), in_=weight_rows)
-        raw_words = []
-        for ir in range(IR):
-            g_raw = raw_pool.tile([P, SLOTS * C], BF16)
-            nc.sync.dma_start(out=g_raw[:], in_=image[ir])
-            raw_words.append(g_raw[:].bitcast(F32))
+        raw = []
+        for gi in range(WINDOW_ROWS):
+            g_raw = work.tile([P, SLOTS * C], BF16)
+            for hi in range(2):
+                nc.sync.dma_start(out=g_raw[hi:P:2, :], in_=blocks[(2 * gi + hi + 1) % BLOCKS])
+            raw.append(g_raw)
 
-        ident2 = const.tile([P, 2 * P], F32)
-        make_identity(nc, ident2[:, 0:P])
-        nc.vector.tensor_copy(out=ident2[:, P : 2 * P], in_=ident2[:, 0:P])
-        identity = ident2[:, 0:P]
-        rotated = ident2[:, 8 : 8 + P].rearrange("p (gi hi a) -> p gi a hi", hi=2, a=8)
-        order_same = const.tile([P, P], F32)
-        nc.vector.tensor_copy(
-            out=order_same[:].rearrange("p (gi gj hi) -> p gi gj hi", gj=8, hi=2), in_=rotated
-        )
-        order_left = const.tile([P, P], F32)
-        left_view = order_left[:].rearrange("p (gi gj hi) -> p gi gj hi", gj=8, hi=2)
-        nc.vector.tensor_copy(out=left_view[:, :, 0:7, :], in_=rotated[:, :, 1:8, :])
-        nc.vector.tensor_copy(out=left_view[:, :, 7:8, :], in_=rotated[:, :, 0:1, :])
+        identity = const.tile([P, P], F32)
+        make_identity(nc, identity[:])
+        order = const.tile([P, P], F32)
+        by_jb = identity[:].rearrange("p (ir gs par hi) -> p par gs hi ir", ir=4, gs=8, par=2)
+        by_w = order[:].rearrange("p (gj hi ir hj) -> p hj gj hi ir", gj=8, hi=2, ir=4)
+        nc.vector.tensor_copy(out=by_w[:, 0], in_=by_jb[:, 1])
+        nc.vector.tensor_copy(out=by_w[:, 1, 0:7], in_=by_jb[:, 0, 1:8])
+        nc.vector.tensor_copy(out=by_w[:, 1, 7:8], in_=by_jb[:, 0, 0:1])
 
-        groups = []
-        for ir in range(IR):
-            groups.append((ir, 4, 0, order_same))
-            groups.append((ir, 0, 4, order_left))
-
-        def turn(g):
-            ir, first_slot, first_tj, order = groups[g]
-            return turn_group(nc, turn_banks, raw_words[ir], first_slot, order[:])
-
-        w_turned = turn_group(nc, turn_banks, w_raw[:].bitcast(F32), 0, identity)
-        turned = {0: turn(0)}
+        w_turned = turn(nc, turn_banks, w_raw, identity[:])
+        turned = {0: turn(nc, turn_banks, raw[0], order[:])}
         w_grouped = const.tile([P, F * PACK], BF16, align_bytes=64)
         regroup(nc, w_turned, w_grouped)
-        turned[1] = turn(1)
+        turned[1] = turn(nc, turn_banks, raw[1], order[:])
         grouped = {}
-        g_grouped = group_pool.tile([P, GROUP * P * PACK], BF16, align_bytes=64)
+        g_grouped = work.tile([P, SLOTS * P * PACK], BF16, align_bytes=64)
         regroup(nc, turned[0], g_grouped)
         grouped[0] = g_grouped
         w_codes = const.tile([P, F], U32, align_bytes=64)
         w_scales = const.tile([P, F], U8, align_bytes=64)
         nc.vector.quantize_mx(out=w_codes[:].bitcast(E4M3X4), scales=w_scales[:], in_=w_grouped[:])
 
-        for g in range(len(groups)):
-            ir, first_slot, first_tj, order = groups[g]
-            if g + 2 < len(groups):
-                turned[g + 2] = turn(g + 2)
-            if g + 1 < len(groups):
-                g_grouped = group_pool.tile([P, GROUP * P * PACK], BF16, align_bytes=64)
-                regroup(nc, turned[g + 1], g_grouped)
-                grouped[g + 1] = g_grouped
-            g_codes = group_pool.tile([P, GROUP * P], U32, align_bytes=64)
-            g_scales = group_pool.tile([P, GROUP * P], U8, align_bytes=64)
+        for gi in range(WINDOW_ROWS):
+            if gi + 2 < WINDOW_ROWS:
+                turned[gi + 2] = turn(nc, turn_banks, raw[gi + 2], order[:])
+            if gi + 1 < WINDOW_ROWS:
+                g_grouped = work.tile([P, SLOTS * P * PACK], BF16, align_bytes=64)
+                regroup(nc, turned[gi + 1], g_grouped)
+                grouped[gi + 1] = g_grouped
+            g_codes = work.tile([P, SLOTS * P], U32, align_bytes=64)
+            g_scales = work.tile([P, SLOTS * P], U8, align_bytes=64)
             nc.vector.quantize_mx(
-                out=g_codes[:].bitcast(E5M2X4), scales=g_scales[:], in_=grouped[g][:]
+                out=g_codes[:].bitcast(E5M2X4), scales=g_scales[:], in_=grouped[gi][:]
             )
-            result = group_pool.tile([P, GROUP * F], F32)
-            for k in range(GROUP):
-                tokens = slice(k * P, (k + 1) * P)
+            result = work.tile([P, SLOTS * F], F32)
+            for jr in range(SLOTS):
+                tokens = slice(jr * P, (jr + 1) * P)
                 sums = sum_banks.tile([P, F], F32)
                 nc.tensor.matmul_mx(
                     out=sums[:],
@@ -135,7 +122,5 @@ def tile_windowattentionblock_pb_kernel(tc, attn_ctx, x, wo, bo, grad_out, out):
                     start=True,
                     stop=True,
                 )
-                nc.scalar.copy(out=result[:, k * F : (k + 1) * F], in_=sums[:])
-            nc.sync.dma_start(
-                out=windows[:, ir, first_tj * F : (first_tj + GROUP) * F], in_=result[:]
-            )
+                nc.scalar.copy(out=result[:, jr * F : (jr + 1) * F], in_=sums[:])
+            nc.sync.dma_start(out=window_rows[gi], in_=result[:])

@@ -39,11 +39,11 @@ def turn(nc, banks, rows, order):
     return turned_banks
 
 
-def regroup(nc, turned_banks, grouped):
+def regroup(copy, turned_banks, grouped):
     grouped_words = grouped[:].bitcast(F32)
     width = BANK_SLOTS * P * HALVES
     for b, turned in enumerate(turned_banks):
-        nc.vector.tensor_copy(
+        copy(
             out=grouped_words[:, b * width : (b + 1) * width].rearrange(
                 "p (k t u) -> p k t u", k=BANK_SLOTS, u=HALVES
             ),
@@ -85,30 +85,27 @@ def tile_windowattentionblock_pb_kernel(tc, attn_ctx, x, wo, bo, grad_out, out):
         nc.vector.tensor_copy(out=by_w[:, 1, 7:8], in_=by_jb[:, 0, 0:1])
 
         w_turned = turn(nc, turn_banks, w_raw, identity[:])
-        turned = {0: turn(nc, turn_banks, raw[0], order[:])}
         w_grouped = const.tile([P, F * PACK], BF16, align_bytes=64)
-        regroup(nc, w_turned, w_grouped)
-        turned[1] = turn(nc, turn_banks, raw[1], order[:])
-        grouped = {}
-        g_grouped = work.tile([P, SLOTS * P * PACK], BF16, align_bytes=64)
-        regroup(nc, turned[0], g_grouped)
-        grouped[0] = g_grouped
+        regroup(nc.scalar.copy, w_turned, w_grouped)
         w_codes = const.tile([P, F], U32, align_bytes=64)
         w_scales = const.tile([P, F], U8, align_bytes=64)
         nc.vector.quantize_mx(out=w_codes[:].bitcast(E4M3X4), scales=w_scales[:], in_=w_grouped[:])
 
+        g_turned = turn(nc, turn_banks, raw[0], order[:])
+        g_grouped = work.tile([P, SLOTS * P * PACK], BF16, align_bytes=64)
+        regroup(nc.scalar.copy, g_turned, g_grouped)
+
         for gi in range(WINDOW_ROWS):
-            if gi + 2 < WINDOW_ROWS:
-                turned[gi + 2] = turn(nc, turn_banks, raw[gi + 2], order[:])
             if gi + 1 < WINDOW_ROWS:
-                g_grouped = work.tile([P, SLOTS * P * PACK], BF16, align_bytes=64)
-                regroup(nc, turned[gi + 1], g_grouped)
-                grouped[gi + 1] = g_grouped
+                g_turned = turn(nc, turn_banks, raw[gi + 1], order[:])
             g_codes = work.tile([P, SLOTS * P], U32, align_bytes=64)
             g_scales = work.tile([P, SLOTS * P], U8, align_bytes=64)
             nc.vector.quantize_mx(
-                out=g_codes[:].bitcast(E5M2X4), scales=g_scales[:], in_=grouped[gi][:]
+                out=g_codes[:].bitcast(E5M2X4), scales=g_scales[:], in_=g_grouped[:]
             )
+            if gi + 1 < WINDOW_ROWS:
+                g_grouped = work.tile([P, SLOTS * P * PACK], BF16, align_bytes=64)
+                regroup(nc.vector.tensor_copy, g_turned, g_grouped)
             result = work.tile([P, SLOTS * F], F32)
             for jr in range(SLOTS):
                 tokens = slice(jr * P, (jr + 1) * P)
@@ -122,5 +119,8 @@ def tile_windowattentionblock_pb_kernel(tc, attn_ctx, x, wo, bo, grad_out, out):
                     start=True,
                     stop=True,
                 )
-                nc.scalar.copy(out=result[:, jr * F : (jr + 1) * F], in_=sums[:])
+                if gi % 2 == 1 and jr == SLOTS - 1:
+                    nc.vector.tensor_copy(out=result[:, jr * F : (jr + 1) * F], in_=sums[:])
+                else:
+                    nc.scalar.copy(out=result[:, jr * F : (jr + 1) * F], in_=sums[:])
             nc.sync.dma_start(out=window_rows[gi], in_=result[:])

@@ -22,6 +22,10 @@ BLOCKS = 16
 SLOTS = 4
 BANK_SLOTS = 2
 
+AHEAD = 2
+TURN_BANKS = 4
+SUM_BANKS = 4
+
 FLOPS = 2 * PIXELS * C * F
 BYTES = 2 * (PIXELS * C + F * C) + 4 * PIXELS * F
 
@@ -39,16 +43,15 @@ def turn(nc, banks, rows, order):
     return turned_banks
 
 
-def regroup(copy, turned_banks, grouped):
+def regroup(copy, turned_banks, grouped, b):
     grouped_words = grouped[:].bitcast(F32)
     width = BANK_SLOTS * P * HALVES
-    for b, turned in enumerate(turned_banks):
-        copy(
-            out=grouped_words[:, b * width : (b + 1) * width].rearrange(
-                "p (k t u) -> p k t u", k=BANK_SLOTS, u=HALVES
-            ),
-            in_=turned[:].rearrange("p k u t -> p k t u"),
-        )
+    copy(
+        out=grouped_words[:, b * width : (b + 1) * width].rearrange(
+            "p (k t u) -> p k t u", k=BANK_SLOTS, u=HALVES
+        ),
+        in_=turned_banks[b][:].rearrange("p k u t -> p k t u"),
+    )
 
 
 def tile_windowattentionblock_pb_kernel(tc, attn_ctx, x, wo, bo, grad_out, out):
@@ -63,8 +66,8 @@ def tile_windowattentionblock_pb_kernel(tc, attn_ctx, x, wo, bo, grad_out, out):
         stack.enter_context(tc.manual_schedule())
         const = stack.enter_context(tc.tile_pool(name="const", bufs=1))
         work = stack.enter_context(tc.tile_pool(name="work", bufs=WINDOW_ROWS))
-        turn_banks = stack.enter_context(tc.psum_pool(name="turn_banks", bufs=4))
-        sum_banks = stack.enter_context(tc.psum_pool(name="sum_banks", bufs=4))
+        turn_banks = stack.enter_context(tc.psum_pool(name="turn_banks", bufs=TURN_BANKS))
+        sum_banks = stack.enter_context(tc.psum_pool(name="sum_banks", bufs=SUM_BANKS))
 
         w_raw = const.tile([P, SLOTS * C], BF16)
         nc.sync.dma_start(out=w_raw[:].rearrange("p (r c) -> p r c", c=C), in_=weight_rows)
@@ -84,42 +87,60 @@ def tile_windowattentionblock_pb_kernel(tc, attn_ctx, x, wo, bo, grad_out, out):
         nc.vector.tensor_copy(out=by_w[:, 1, 0:7], in_=by_jb[:, 0, 1:8])
         nc.vector.tensor_copy(out=by_w[:, 1, 7:8], in_=by_jb[:, 0, 0:1])
 
-        w_turned = turn(nc, turn_banks, w_raw, identity[:])
-        w_grouped = const.tile([P, F * PACK], BF16, align_bytes=64)
-        regroup(nc.scalar.copy, w_turned, w_grouped)
-        w_codes = const.tile([P, F], U32, align_bytes=64)
-        w_scales = const.tile([P, F], U8, align_bytes=64)
-        nc.vector.quantize_mx(out=w_codes[:].bitcast(E4M3X4), scales=w_scales[:], in_=w_grouped[:])
+        turned = {}
+        grouped = {}
+        codes = {}
+        scales = {}
 
-        g_turned = turn(nc, turn_banks, raw[0], order[:])
-        g_grouped = work.tile([P, SLOTS * P * PACK], BF16, align_bytes=64)
-        regroup(nc.scalar.copy, g_turned, g_grouped)
+        def transpose_row(gi):
+            turned[gi] = turn(nc, turn_banks, raw[gi], order[:])
+            g_grouped = work.tile([P, SLOTS * P * PACK], BF16, align_bytes=64)
+            grouped[gi] = g_grouped
 
-        for gi in range(WINDOW_ROWS):
-            if gi + 1 < WINDOW_ROWS:
-                g_turned = turn(nc, turn_banks, raw[gi + 1], order[:])
+        def quantise_row(gi):
             g_codes = work.tile([P, SLOTS * P], U32, align_bytes=64)
             g_scales = work.tile([P, SLOTS * P], U8, align_bytes=64)
             nc.vector.quantize_mx(
-                out=g_codes[:].bitcast(E5M2X4), scales=g_scales[:], in_=g_grouped[:]
+                out=g_codes[:].bitcast(E5M2X4), scales=g_scales[:], in_=grouped[gi][:]
             )
+            codes[gi] = g_codes
+            scales[gi] = g_scales
+
+        w_turned = turn(nc, turn_banks, w_raw, identity[:])
+        w_grouped = const.tile([P, F * PACK], BF16, align_bytes=64)
+        regroup(nc.scalar.copy, w_turned, w_grouped, 0)
+        regroup(nc.scalar.copy, w_turned, w_grouped, 1)
+        w_codes = const.tile([P, F], U32, align_bytes=64)
+        w_scales = const.tile([P, F], U8, align_bytes=64)
+        nc.vector.quantize_mx(out=w_codes[:].bitcast(E4M3X4), scales=w_scales[:], in_=w_grouped[:])
+        for gi in range(AHEAD):
+            transpose_row(gi)
+            regroup(nc.scalar.copy, turned[gi], grouped[gi], 0)
+            regroup(nc.scalar.copy, turned[gi], grouped[gi], 1)
+        quantise_row(0)
+
+        for gi in range(WINDOW_ROWS):
+            if gi + AHEAD < WINDOW_ROWS:
+                transpose_row(gi + AHEAD)
+                regroup(nc.vector.tensor_copy, turned[gi + AHEAD], grouped[gi + AHEAD], 0)
             if gi + 1 < WINDOW_ROWS:
-                g_grouped = work.tile([P, SLOTS * P * PACK], BF16, align_bytes=64)
-                regroup(nc.vector.tensor_copy, g_turned, g_grouped)
+                quantise_row(gi + 1)
+            if gi + AHEAD < WINDOW_ROWS:
+                regroup(nc.vector.tensor_copy, turned[gi + AHEAD], grouped[gi + AHEAD], 1)
             result = work.tile([P, SLOTS * F], F32)
             for jr in range(SLOTS):
                 tokens = slice(jr * P, (jr + 1) * P)
                 sums = sum_banks.tile([P, F], F32)
                 nc.tensor.matmul_mx(
                     out=sums[:],
-                    lhsT=g_codes[:, tokens].bitcast(E5M2X4),
-                    lhsT_scale=g_scales[:, tokens],
+                    lhsT=codes[gi][:, tokens].bitcast(E5M2X4),
+                    lhsT_scale=scales[gi][:, tokens],
                     rhs=w_codes[:].bitcast(E4M3X4),
                     rhs_scale=w_scales[:],
                     start=True,
                     stop=True,
                 )
-                if gi % 2 == 1 and jr == SLOTS - 1:
+                if gi % 2 == 1 and jr == 0:
                     nc.vector.tensor_copy(out=result[:, jr * F : (jr + 1) * F], in_=sums[:])
                 else:
                     nc.scalar.copy(out=result[:, jr * F : (jr + 1) * F], in_=sums[:])

@@ -22,7 +22,7 @@ BLOCKS = 16
 SLOTS = 4
 BANK_SLOTS = 2
 
-AHEAD = 2
+VECTOR_BANKS = ((1, 3), (0,), (), (0,), (), (0,), (1, 3), (1, 3))
 TURN_BANKS = 4
 SUM_BANKS = 4
 
@@ -97,36 +97,30 @@ def tile_windowattentionblock_pb_kernel(tc, attn_ctx, x, wo, bo, grad_out, out):
             g_grouped = work.tile([P, SLOTS * P * PACK], BF16, align_bytes=64)
             grouped[gi] = g_grouped
 
-        def quantise_row(gi):
+        def new_codes(gi):
             g_codes = work.tile([P, SLOTS * P], U32, align_bytes=64)
             g_scales = work.tile([P, SLOTS * P], U8, align_bytes=64)
-            nc.vector.quantize_mx(
-                out=g_codes[:].bitcast(E5M2X4), scales=g_scales[:], in_=grouped[gi][:]
-            )
             codes[gi] = g_codes
             scales[gi] = g_scales
 
-        w_turned = turn(nc, turn_banks, w_raw, identity[:])
-        w_grouped = const.tile([P, F * PACK], BF16, align_bytes=64)
-        regroup(nc.scalar.copy, w_turned, w_grouped, 0)
-        regroup(nc.scalar.copy, w_turned, w_grouped, 1)
-        w_codes = const.tile([P, F], U32, align_bytes=64)
-        w_scales = const.tile([P, F], U8, align_bytes=64)
-        nc.vector.quantize_mx(out=w_codes[:].bitcast(E4M3X4), scales=w_scales[:], in_=w_grouped[:])
-        for gi in range(AHEAD):
-            transpose_row(gi)
-            regroup(nc.scalar.copy, turned[gi], grouped[gi], 0)
-            regroup(nc.scalar.copy, turned[gi], grouped[gi], 1)
-        quantise_row(0)
+        def quantise(gi, first, last):
+            nc.vector.quantize_mx(
+                out=codes[gi][:, first * P : last * P].bitcast(E5M2X4),
+                scales=scales[gi][:, first * P : last * P],
+                in_=grouped[gi][:, first * P * PACK : last * P * PACK],
+            )
 
-        for gi in range(WINDOW_ROWS):
-            if gi + AHEAD < WINDOW_ROWS:
-                transpose_row(gi + AHEAD)
-                regroup(nc.vector.tensor_copy, turned[gi + AHEAD], grouped[gi + AHEAD], 0)
-            if gi + 1 < WINDOW_ROWS:
-                quantise_row(gi + 1)
-            if gi + AHEAD < WINDOW_ROWS:
-                regroup(nc.vector.tensor_copy, turned[gi + AHEAD], grouped[gi + AHEAD], 1)
+        def prepare(gi):
+            if gi < WINDOW_ROWS:
+                transpose_row(gi)
+                regroup(nc.vector.tensor_copy, turned[gi], grouped[gi], 0)
+            if gi - 1 < WINDOW_ROWS:
+                new_codes(gi - 1)
+                quantise(gi - 1, 0, SLOTS)
+            if gi < WINDOW_ROWS:
+                regroup(nc.vector.tensor_copy, turned[gi], grouped[gi], 1)
+
+        def multiply(gi):
             result = work.tile([P, SLOTS * F], F32)
             for jr in range(SLOTS):
                 tokens = slice(jr * P, (jr + 1) * P)
@@ -140,8 +134,35 @@ def tile_windowattentionblock_pb_kernel(tc, attn_ctx, x, wo, bo, grad_out, out):
                     start=True,
                     stop=True,
                 )
-                if gi % 2 == 1 and jr == 0:
+                if jr in VECTOR_BANKS[gi]:
                     nc.vector.tensor_copy(out=result[:, jr * F : (jr + 1) * F], in_=sums[:])
                 else:
                     nc.scalar.copy(out=result[:, jr * F : (jr + 1) * F], in_=sums[:])
-            nc.sync.dma_start(out=window_rows[gi], in_=result[:])
+                if gi == 0 and jr == 1:
+                    nc.sync.dma_start(out=window_rows[gi][:, : 2 * F], in_=result[:, : 2 * F])
+            if gi == 0:
+                nc.sync.dma_start(out=window_rows[gi][:, 2 * F :], in_=result[:, 2 * F :])
+            else:
+                nc.sync.dma_start(out=window_rows[gi], in_=result[:])
+
+        w_turned = turn(nc, turn_banks, w_raw, identity[:])
+        w_grouped = const.tile([P, F * PACK], BF16, align_bytes=64)
+        regroup(nc.scalar.copy, w_turned, w_grouped, 0)
+        regroup(nc.scalar.copy, w_turned, w_grouped, 1)
+        w_codes = const.tile([P, F], U32, align_bytes=64)
+        w_scales = const.tile([P, F], U8, align_bytes=64)
+        nc.vector.quantize_mx(out=w_codes[:].bitcast(E4M3X4), scales=w_scales[:], in_=w_grouped[:])
+        transpose_row(0)
+        new_codes(0)
+        for b in range(SLOTS // BANK_SLOTS):
+            regroup(nc.scalar.copy, turned[0], grouped[0], b)
+            quantise(0, b * BANK_SLOTS, (b + 1) * BANK_SLOTS)
+        transpose_row(1)
+        regroup(nc.scalar.copy, turned[1], grouped[1], 0)
+        regroup(nc.scalar.copy, turned[1], grouped[1], 1)
+
+        multiply(0)
+        prepare(2)
+        for gi in range(1, WINDOW_ROWS):
+            prepare(gi + 2)
+            multiply(gi)

@@ -17,21 +17,22 @@ PIXELS = 64 * 64
 WORDS = C // 2
 HALVES = WORDS // P
 PACK = 4
-WINDOW_ROWS = 8
+UNITS = 4
+UNIT_BLOCKS = 4
 BLOCKS = 16
+UNIT_SLOTS = 8
+STEPS = 2 * UNITS
 SLOTS = 4
 BANK_SLOTS = 2
-
-VECTOR_BANKS = ((1, 3), (0,), (), (0,), (), (0,), (1, 3), (1, 3))
 TURN_BANKS = 4
 SUM_BANKS = 4
+VECTOR_BANKS = ((1, 3), (0,), (), (0,), (), (0,), (1, 3), (1, 3))
 
 FLOPS = 2 * PIXELS * C * F
 BYTES = 2 * (PIXELS * C + F * C) + 4 * PIXELS * F
 
 
-def turn(nc, banks, rows, order):
-    words = rows[:].bitcast(F32)
+def turn(nc, banks, words, order):
     turned_banks = []
     for b in range(SLOTS // BANK_SLOTS):
         turned = banks.tile([P, BANK_SLOTS, HALVES, P], F32, name="turned")
@@ -56,113 +57,148 @@ def regroup(copy, turned_banks, grouped, b):
 
 def tile_windowattentionblock_pb_kernel(tc, attn_ctx, x, wo, bo, grad_out, out):
     nc = tc.nc
-    blocks = grad_out.rearrange("b (ib ir) (jb jr) c -> (b ib) (ir jb) (jr c)", ir=4, jr=SLOTS)
-    window_rows = out.rearrange(
-        "(gi gj) (hi ir hj jr) h d -> gi (gj hi ir hj) (jr h d)", gi=WINDOW_ROWS, hi=2, ir=4, hj=2
+    blocks = grad_out.rearrange(
+        "b (ib ir) (jc s) c -> (b ib) (ir jc) (s c)", ir=4, s=UNIT_SLOTS
     )
-    weight_rows = wo.rearrange("h d c -> (h d) c").rearrange("(r p) c -> p r c", p=P)
+    units_out = out.rearrange(
+        "(a gl gj) (ti tj) h d -> a (gl gj ti) (tj h d)", a=UNITS, gl=2, ti=8
+    )
+    weight_rows = wo.rearrange("h d c -> (h d) c").rearrange("(p r) c -> p (r c)", p=P)
 
     with ExitStack() as stack:
         stack.enter_context(tc.manual_schedule())
         const = stack.enter_context(tc.tile_pool(name="const", bufs=1))
-        work = stack.enter_context(tc.tile_pool(name="work", bufs=WINDOW_ROWS))
+        units = stack.enter_context(tc.tile_pool(name="units", bufs=UNITS))
+        work = stack.enter_context(tc.tile_pool(name="work", bufs=STEPS))
         turn_banks = stack.enter_context(tc.psum_pool(name="turn_banks", bufs=TURN_BANKS))
         sum_banks = stack.enter_context(tc.psum_pool(name="sum_banks", bufs=SUM_BANKS))
 
         w_raw = const.tile([P, SLOTS * C], BF16)
-        nc.sync.dma_start(out=w_raw[:].rearrange("p (r c) -> p r c", c=C), in_=weight_rows)
+        nc.sync.dma_start(out=w_raw[:], in_=weight_rows)
         raw = []
-        for gi in range(WINDOW_ROWS):
-            g_raw = work.tile([P, SLOTS * C], BF16)
-            for hi in range(2):
-                nc.sync.dma_start(out=g_raw[hi:P:2, :], in_=blocks[(2 * gi + hi + 1) % BLOCKS])
+        half = SLOTS * C
+        for a in range(UNITS):
+            g_raw = units.tile([P, UNIT_SLOTS * C], BF16)
+            first = UNIT_BLOCKS * a + 1
+            if a == 0:
+                for cols in (slice(half, 2 * half), slice(0, half)):
+                    nc.sync.dma_start(
+                        out=g_raw[:, cols],
+                        in_=blocks[first : first + UNIT_BLOCKS, :, cols].rearrange("c q x -> q c x"),
+                    )
+            elif first + UNIT_BLOCKS <= BLOCKS:
+                nc.sync.dma_start(
+                    out=g_raw[:],
+                    in_=blocks[first : first + UNIT_BLOCKS].rearrange("c q x -> q c x"),
+                )
+            else:
+                for c in range(UNIT_BLOCKS):
+                    nc.sync.dma_start(
+                        out=g_raw[c:P:UNIT_BLOCKS, :], in_=blocks[(first + c) % BLOCKS]
+                    )
             raw.append(g_raw)
 
         identity = const.tile([P, P], F32)
         make_identity(nc, identity[:])
-        order = const.tile([P, P], F32)
-        by_jb = identity[:].rearrange("p (ir gs par hi) -> p par gs hi ir", ir=4, gs=8, par=2)
-        by_w = order[:].rearrange("p (gj hi ir hj) -> p hj gj hi ir", gj=8, hi=2, ir=4)
-        nc.vector.tensor_copy(out=by_w[:, 0], in_=by_jb[:, 1])
-        nc.vector.tensor_copy(out=by_w[:, 1, 0:7], in_=by_jb[:, 0, 1:8])
-        nc.vector.tensor_copy(out=by_w[:, 1, 7:8], in_=by_jb[:, 0, 0:1])
+        by_src = identity[:].rearrange("p (ir jc gl ch) -> p gl jc ch ir", ir=4, jc=8, gl=2, ch=2)
+        orders = []
+        for h in range(2):
+            order = const.tile([P, P], F32, name="order%d" % h)
+            by_w = order[:].rearrange("p (gl gj ch ir) -> p gl gj ch ir", gl=2, gj=8, ch=2, ir=4)
+            for gl in range(2):
+                if h == 0:
+                    nc.vector.tensor_copy(out=by_w[:, gl], in_=by_src[:, gl])
+                else:
+                    nc.vector.tensor_copy(out=by_w[:, gl, 0:7], in_=by_src[:, gl, 1:8])
+                    nc.vector.tensor_copy(out=by_w[:, gl, 7:8], in_=by_src[:, gl, 0:1])
+            orders.append(order)
 
         turned = {}
         grouped = {}
         codes = {}
         scales = {}
+        results = {}
 
-        def transpose_row(gi):
-            turned[gi] = turn(nc, turn_banks, raw[gi], order[:])
+        def transpose_step(st):
+            a, h = st // 2, st % 2
+            words = raw[a][:].bitcast(F32)
+            first_word = (1 - h) * SLOTS * WORDS
+            turned[st] = turn(
+                nc, turn_banks, words[:, first_word : first_word + SLOTS * WORDS], orders[h][:]
+            )
             g_grouped = work.tile([P, SLOTS * P * PACK], BF16, align_bytes=64)
-            grouped[gi] = g_grouped
+            grouped[st] = g_grouped
 
-        def new_codes(gi):
+        def new_codes(st):
             g_codes = work.tile([P, SLOTS * P], U32, align_bytes=64)
             g_scales = work.tile([P, SLOTS * P], U8, align_bytes=64)
-            codes[gi] = g_codes
-            scales[gi] = g_scales
+            codes[st] = g_codes
+            scales[st] = g_scales
 
-        def quantise(gi, first, last):
+        def quantise(st, first, last):
             nc.vector.quantize_mx(
-                out=codes[gi][:, first * P : last * P].bitcast(E5M2X4),
-                scales=scales[gi][:, first * P : last * P],
-                in_=grouped[gi][:, first * P * PACK : last * P * PACK],
+                out=codes[st][:, first * P : last * P].bitcast(E5M2X4),
+                scales=scales[st][:, first * P : last * P],
+                in_=grouped[st][:, first * P * PACK : last * P * PACK],
             )
 
-        def prepare(gi):
-            if gi < WINDOW_ROWS:
-                transpose_row(gi)
-                regroup(nc.vector.tensor_copy, turned[gi], grouped[gi], 0)
-            if gi - 1 < WINDOW_ROWS:
-                new_codes(gi - 1)
-                quantise(gi - 1, 0, SLOTS)
-            if gi < WINDOW_ROWS:
-                regroup(nc.vector.tensor_copy, turned[gi], grouped[gi], 1)
+        def prepare(st):
+            if st < STEPS:
+                transpose_step(st)
+                regroup(nc.vector.tensor_copy, turned[st], grouped[st], 0)
+            if st - 1 < STEPS:
+                new_codes(st - 1)
+                quantise(st - 1, 0, SLOTS)
+            if st < STEPS:
+                regroup(nc.vector.tensor_copy, turned[st], grouped[st], 1)
 
-        def multiply(gi):
-            result = work.tile([P, SLOTS * F], F32)
-            for jr in range(SLOTS):
-                tokens = slice(jr * P, (jr + 1) * P)
+        def multiply(st):
+            a, h = st // 2, st % 2
+            if h == 0:
+                result = units.tile([P, UNIT_SLOTS * F], F32)
+                results[a] = result
+            result = results[a]
+            for j in range(SLOTS):
+                tokens = slice(j * P, (j + 1) * P)
                 sums = sum_banks.tile([P, F], F32)
                 nc.tensor.matmul_mx(
                     out=sums[:],
-                    lhsT=codes[gi][:, tokens].bitcast(E5M2X4),
-                    lhsT_scale=scales[gi][:, tokens],
+                    lhsT=codes[st][:, tokens].bitcast(E5M2X4),
+                    lhsT_scale=scales[st][:, tokens],
                     rhs=w_codes[:].bitcast(E4M3X4),
                     rhs_scale=w_scales[:],
                     start=True,
                     stop=True,
                 )
-                if jr in VECTOR_BANKS[gi]:
-                    nc.vector.tensor_copy(out=result[:, jr * F : (jr + 1) * F], in_=sums[:])
+                tj = SLOTS * h + j
+                if j in VECTOR_BANKS[st]:
+                    nc.vector.tensor_copy(out=result[:, tj * F : (tj + 1) * F], in_=sums[:])
                 else:
-                    nc.scalar.copy(out=result[:, jr * F : (jr + 1) * F], in_=sums[:])
-                if gi == 0 and jr == 1:
-                    nc.sync.dma_start(out=window_rows[gi][:, : 2 * F], in_=result[:, : 2 * F])
-            if gi == 0:
-                nc.sync.dma_start(out=window_rows[gi][:, 2 * F :], in_=result[:, 2 * F :])
-            else:
-                nc.sync.dma_start(out=window_rows[gi], in_=result[:])
+                    nc.scalar.copy(out=result[:, tj * F : (tj + 1) * F], in_=sums[:])
+            cols = slice(SLOTS * h * F, SLOTS * (h + 1) * F)
+            nc.sync.dma_start(out=units_out[a][:, cols], in_=result[:, cols])
 
-        w_turned = turn(nc, turn_banks, w_raw, identity[:])
+        w_turned = turn(nc, turn_banks, w_raw[:].bitcast(F32), identity[:])
         w_grouped = const.tile([P, F * PACK], BF16, align_bytes=64)
-        regroup(nc.scalar.copy, w_turned, w_grouped, 0)
-        regroup(nc.scalar.copy, w_turned, w_grouped, 1)
+        w_words = w_grouped[:].bitcast(F32).rearrange(
+            "p (t b k u) -> p b t k u", b=SLOTS // BANK_SLOTS, k=BANK_SLOTS, u=HALVES
+        )
+        for b in range(SLOTS // BANK_SLOTS):
+            nc.scalar.copy(out=w_words[:, b], in_=w_turned[b][:].rearrange("p k u t -> p t k u"))
         w_codes = const.tile([P, F], U32, align_bytes=64)
         w_scales = const.tile([P, F], U8, align_bytes=64)
         nc.vector.quantize_mx(out=w_codes[:].bitcast(E4M3X4), scales=w_scales[:], in_=w_grouped[:])
-        transpose_row(0)
+        transpose_step(0)
         new_codes(0)
         for b in range(SLOTS // BANK_SLOTS):
             regroup(nc.scalar.copy, turned[0], grouped[0], b)
             quantise(0, b * BANK_SLOTS, (b + 1) * BANK_SLOTS)
-        transpose_row(1)
+        transpose_step(1)
         regroup(nc.scalar.copy, turned[1], grouped[1], 0)
         regroup(nc.scalar.copy, turned[1], grouped[1], 1)
 
         multiply(0)
         prepare(2)
-        for gi in range(1, WINDOW_ROWS):
-            prepare(gi + 2)
-            multiply(gi)
+        for st in range(1, STEPS):
+            prepare(st + 2)
+            multiply(st)

from contextlib import ExitStack

import concourse.mybir as mybir
from concourse.masks import make_identity

BF16 = mybir.dt.bfloat16
F32 = mybir.dt.float32
U32 = mybir.dt.uint32
U8 = mybir.dt.uint8
E4M3X4 = mybir.dt.float8_e4m3fn_x4
E5M2X4 = mybir.dt.float8_e5m2_x4

P = 128
C = 512
F = 512
PIXELS = 64 * 64
WORDS = C // 2
HALVES = WORDS // P
PACK = 4
UNITS = 4
UNIT_BLOCKS = 4
BLOCKS = 16
UNIT_SLOTS = 8
STEPS = 2 * UNITS
SLOTS = 4
BANK_SLOTS = 2
TURN_BANKS = 4
SUM_BANKS = 4
VECTOR_BANKS = ((1, 3), (0,), (), (0,), (), (0,), (1, 3), (1, 3))

FLOPS = 2 * PIXELS * C * F
BYTES = 2 * (PIXELS * C + F * C) + 4 * PIXELS * F


def turn(nc, banks, words, order):
    turned_banks = []
    for b in range(SLOTS // BANK_SLOTS):
        turned = banks.tile([P, BANK_SLOTS, HALVES, P], F32, name="turned")
        for k in range(BANK_SLOTS):
            for u in range(HALVES):
                start = (b * BANK_SLOTS + k) * WORDS + u * P
                nc.tensor.transpose(turned[:, k, u, :], words[:, start : start + P], order)
        turned_banks.append(turned)
    return turned_banks


def regroup(copy, turned_banks, grouped, b):
    grouped_words = grouped[:].bitcast(F32)
    width = BANK_SLOTS * P * HALVES
    copy(
        out=grouped_words[:, b * width : (b + 1) * width].rearrange(
            "p (k t u) -> p k t u", k=BANK_SLOTS, u=HALVES
        ),
        in_=turned_banks[b][:].rearrange("p k u t -> p k t u"),
    )


def tile_windowattentionblock_pb_kernel(tc, attn_ctx, x, wo, bo, grad_out, out):
    nc = tc.nc
    blocks = grad_out.rearrange(
        "b (ib ir) (jc s) c -> (b ib) (ir jc) (s c)", ir=4, s=UNIT_SLOTS
    )
    units_out = out.rearrange(
        "(a gl gj) (ti tj) h d -> a (gl gj ti) (tj h d)", a=UNITS, gl=2, ti=8
    )
    weight_rows = wo.rearrange("h d c -> (h d) c").rearrange("(p r) c -> p (r c)", p=P)

    with ExitStack() as stack:
        stack.enter_context(tc.manual_schedule())
        const = stack.enter_context(tc.tile_pool(name="const", bufs=1))
        units = stack.enter_context(tc.tile_pool(name="units", bufs=UNITS))
        work = stack.enter_context(tc.tile_pool(name="work", bufs=STEPS))
        turn_banks = stack.enter_context(tc.psum_pool(name="turn_banks", bufs=TURN_BANKS))
        sum_banks = stack.enter_context(tc.psum_pool(name="sum_banks", bufs=SUM_BANKS))

        w_raw = const.tile([P, SLOTS * C], BF16)
        nc.sync.dma_start(out=w_raw[:], in_=weight_rows)
        raw = []
        half = SLOTS * C
        for a in range(UNITS):
            g_raw = units.tile([P, UNIT_SLOTS * C], BF16)
            first = UNIT_BLOCKS * a + 1
            if a == 0:
                for cols in (slice(half, 2 * half), slice(0, half)):
                    nc.sync.dma_start(
                        out=g_raw[:, cols],
                        in_=blocks[first : first + UNIT_BLOCKS, :, cols].rearrange("c q x -> q c x"),
                    )
            elif first + UNIT_BLOCKS <= BLOCKS:
                nc.sync.dma_start(
                    out=g_raw[:],
                    in_=blocks[first : first + UNIT_BLOCKS].rearrange("c q x -> q c x"),
                )
            else:
                for c in range(UNIT_BLOCKS):
                    nc.sync.dma_start(
                        out=g_raw[c:P:UNIT_BLOCKS, :], in_=blocks[(first + c) % BLOCKS]
                    )
            raw.append(g_raw)

        identity = const.tile([P, P], F32)
        make_identity(nc, identity[:])
        by_src = identity[:].rearrange("p (ir jc gl ch) -> p gl jc ch ir", ir=4, jc=8, gl=2, ch=2)
        orders = []
        for h in range(2):
            order = const.tile([P, P], F32, name="order%d" % h)
            by_w = order[:].rearrange("p (gl gj ch ir) -> p gl gj ch ir", gl=2, gj=8, ch=2, ir=4)
            for gl in range(2):
                if h == 0:
                    nc.vector.tensor_copy(out=by_w[:, gl], in_=by_src[:, gl])
                else:
                    nc.vector.tensor_copy(out=by_w[:, gl, 0:7], in_=by_src[:, gl, 1:8])
                    nc.vector.tensor_copy(out=by_w[:, gl, 7:8], in_=by_src[:, gl, 0:1])
            orders.append(order)

        turned = {}
        grouped = {}
        codes = {}
        scales = {}
        results = {}

        def transpose_step(st):
            a, h = st // 2, st % 2
            words = raw[a][:].bitcast(F32)
            first_word = (1 - h) * SLOTS * WORDS
            turned[st] = turn(
                nc, turn_banks, words[:, first_word : first_word + SLOTS * WORDS], orders[h][:]
            )
            g_grouped = work.tile([P, SLOTS * P * PACK], BF16, align_bytes=64)
            grouped[st] = g_grouped

        def new_codes(st):
            g_codes = work.tile([P, SLOTS * P], U32, align_bytes=64)
            g_scales = work.tile([P, SLOTS * P], U8, align_bytes=64)
            codes[st] = g_codes
            scales[st] = g_scales

        def quantise(st, first, last):
            nc.vector.quantize_mx(
                out=codes[st][:, first * P : last * P].bitcast(E5M2X4),
                scales=scales[st][:, first * P : last * P],
                in_=grouped[st][:, first * P * PACK : last * P * PACK],
            )

        def prepare(st):
            if st < STEPS:
                transpose_step(st)
                regroup(nc.vector.tensor_copy, turned[st], grouped[st], 0)
            if st - 1 < STEPS:
                new_codes(st - 1)
                quantise(st - 1, 0, SLOTS)
            if st < STEPS:
                regroup(nc.vector.tensor_copy, turned[st], grouped[st], 1)

        def multiply(st):
            a, h = st // 2, st % 2
            if h == 0:
                result = units.tile([P, UNIT_SLOTS * F], F32)
                results[a] = result
            result = results[a]
            for j in range(SLOTS):
                tokens = slice(j * P, (j + 1) * P)
                sums = sum_banks.tile([P, F], F32)
                nc.tensor.matmul_mx(
                    out=sums[:],
                    lhsT=codes[st][:, tokens].bitcast(E5M2X4),
                    lhsT_scale=scales[st][:, tokens],
                    rhs=w_codes[:].bitcast(E4M3X4),
                    rhs_scale=w_scales[:],
                    start=True,
                    stop=True,
                )
                tj = SLOTS * h + j
                if j in VECTOR_BANKS[st]:
                    nc.vector.tensor_copy(out=result[:, tj * F : (tj + 1) * F], in_=sums[:])
                else:
                    nc.scalar.copy(out=result[:, tj * F : (tj + 1) * F], in_=sums[:])
            cols = slice(SLOTS * h * F, SLOTS * (h + 1) * F)
            nc.sync.dma_start(out=units_out[a][:, cols], in_=result[:, cols])

        w_turned = turn(nc, turn_banks, w_raw[:].bitcast(F32), identity[:])
        w_grouped = const.tile([P, F * PACK], BF16, align_bytes=64)
        w_words = w_grouped[:].bitcast(F32).rearrange(
            "p (t b k u) -> p b t k u", b=SLOTS // BANK_SLOTS, k=BANK_SLOTS, u=HALVES
        )
        for b in range(SLOTS // BANK_SLOTS):
            nc.scalar.copy(out=w_words[:, b], in_=w_turned[b][:].rearrange("p k u t -> p t k u"))
        w_codes = const.tile([P, F], U32, align_bytes=64)
        w_scales = const.tile([P, F], U8, align_bytes=64)
        nc.vector.quantize_mx(out=w_codes[:].bitcast(E4M3X4), scales=w_scales[:], in_=w_grouped[:])
        transpose_step(0)
        new_codes(0)
        for b in range(SLOTS // BANK_SLOTS):
            regroup(nc.scalar.copy, turned[0], grouped[0], b)
            quantise(0, b * BANK_SLOTS, (b + 1) * BANK_SLOTS)
        transpose_step(1)
        regroup(nc.scalar.copy, turned[1], grouped[1], 0)
        regroup(nc.scalar.copy, turned[1], grouped[1], 1)

        multiply(0)
        prepare(2)
        for st in range(1, STEPS):
            prepare(st + 2)
            multiply(st)
